import numpy as np
import ml_dtypes


def mxq(x, axis, fmt="e4m3"):
    dtype, down = {"e4m3": (ml_dtypes.float8_e4m3fn, 7), "e5m2": (ml_dtypes.float8_e5m2, 14)}[fmt]
    v = np.moveaxis(np.asarray(x, np.float32).astype(ml_dtypes.bfloat16).astype(np.float64), axis, -1)
    blocks = v.reshape(v.shape[:-1] + (-1, 32))
    amax = np.abs(blocks).max(-1, keepdims=True)
    byte = np.maximum(np.where(amax > 0, np.frexp(amax)[1] - 1 + 127, 0) - down, 1)
    scale = np.exp2(byte - 127.0)
    codes = (blocks / scale).astype(np.float32).astype(dtype).astype(np.float64)
    return np.moveaxis((codes * scale).reshape(v.shape), -1, axis)


WIDE = False


def mx_kscale(k):
    if not WIDE:
        return np.ones(k)
    levels = np.array([20, -20, 10, -10, 0])
    a = np.random.permutation(np.resize(levels, k // 512 * 4)).reshape(k // 512, 4)
    idx = np.arange(k)
    return np.exp2(a[idx // 512, idx % 128 // 32])


BF16 = ml_dtypes.bfloat16


def bf(x):
    return np.asarray(x, np.float32).astype(BF16)


def f64(x):
    return np.asarray(x).astype(np.float64)


N, LMAX, CIN, COUT = 512, 3, 1024, 512
NL = LMAX + 1
NM = NL * NL


def setup_inputs():
    s = mx_kscale(NM * N).reshape(NM, N).T[:, :, None]
    x = np.random.standard_normal((N, NM, CIN)) * s
    weights = np.random.standard_normal((NL, CIN, COUT)) / np.sqrt(CIN)
    path_weights = 1.0 + 0.3 * np.random.standard_normal(NL)
    g = np.random.standard_normal((N, NM, COUT)) * np.exp2(np.random.randint(-12, 1, (N, NM, 1))) / s
    return {"x": bf(x), "weights": bf(weights), "path_weights": bf(path_weights), "grad_out": bf(g)}


def degree_tokens(a, l):
    blk = a[:, l * l:(l + 1) * (l + 1), :]
    return blk.transpose(1, 0, 2).reshape(-1, a.shape[2])


def reference(x, weights, path_weights, grad_out):
    x, path_weights, g = f64(x), f64(path_weights), f64(grad_out)
    grads = []
    for l in range(NL):
        xl = mxq(degree_tokens(x, l), 0, "e4m3")
        gl = mxq(degree_tokens(g, l), 0, "e5m2")
        grads.append(path_weights[l] * (xl.T @ gl))
    return np.stack(grads, axis=0)

@@ -1,0 +1,135 @@
+from contextlib import ExitStack
+
+import concourse.mybir as mybir
+
+BF16 = mybir.dt.bfloat16
+F32 = mybir.dt.float32
+U32 = mybir.dt.uint32
+U8 = mybir.dt.uint8
+E4M3_X4 = mybir.dt.float8_e4m3fn_x4
+E5M2_X4 = mybir.dt.float8_e5m2_x4
+COPY = mybir.ActivationFunctionType.Copy
+
+P = 128
+PACK = 4
+NODES = P * PACK
+DEGREES = 4
+C_IN = 1024
+C_OUT = 512
+IN_TILES = C_IN // P
+RUN = 4
+
+M_CHUNK = 3
+RAW_BUFS = 4
+STORE_TILES = 2
+LAST_PIECES = 4
+
+FLOPS = 2 * NODES * DEGREES * DEGREES * C_IN * C_OUT
+BYTES = 2 * NODES * DEGREES * DEGREES * (C_IN + C_OUT) + 4 * DEGREES * C_IN * C_OUT + 2 * DEGREES
+
+
+def regroup(copy, grouped, raw_row):
+    copy(
+        out=grouped.rearrange("p (c i) j -> p c j i", i=RUN),
+        in_=raw_row.rearrange("p j (c i) -> p c j i", i=RUN),
+    )
+
+
+def tile_linear_pa_kernel(tc, x, weights, path_weights, grad_out, out):
+    nc = tc.nc
+    x_nodes = x.rearrange("(p j) m c -> p j m c", j=PACK)
+    g_nodes = grad_out.rearrange("(p j) m c -> p j m c", j=PACK)
+
+    rows = []
+    for l in range(DEGREES):
+        for m in range(l * l, (l + 1) * (l + 1)):
+            rows.append((l, m, m == l * l, m == (l + 1) * (l + 1) - 1))
+    last_step = len(rows) - 1
+
+    with ExitStack() as ctx:
+        consts = ctx.enter_context(tc.tile_pool(name="consts", bufs=1))
+        raw = ctx.enter_context(tc.tile_pool(name="raw", bufs=RAW_BUFS))
+        side = ctx.enter_context(tc.tile_pool(name="side", bufs=3))
+        packed = ctx.enter_context(tc.tile_pool(name="packed", bufs=3))
+        staging = ctx.enter_context(tc.tile_pool(name="staging", bufs=4))
+        banks = ctx.enter_context(tc.psum_pool(name="banks", bufs=IN_TILES))
+
+        pw_bf16 = consts.tile([P, DEGREES], BF16)
+        nc.scalar.dma_start(out=pw_bf16[:], in_=path_weights.partition_broadcast(P))
+        pw = consts.tile([P, DEGREES], F32)
+        nc.vector.tensor_copy(out=pw[:], in_=pw_bf16[:])
+
+        raw_of_row = {}
+        grouped_of_step = {}
+        acc_of_degree = {}
+
+        def load_chunk(m_first, count):
+            x_raw = raw.tile([P, PACK, count, C_IN], BF16, tag="x_raw")
+            nc.sync.dma_start(out=x_raw[:], in_=x_nodes[:, :, m_first : m_first + count, :])
+            g_raw = raw.tile([P, PACK, count, C_OUT], BF16, tag="g_raw")
+            nc.sync.dma_start(out=g_raw[:], in_=g_nodes[:, :, m_first : m_first + count, :])
+            for k in range(count):
+                raw_of_row[m_first + k] = (x_raw, g_raw, k)
+
+        def pieces_of(step):
+            return LAST_PIECES if step == last_step else 1
+
+        def regroup_step(step):
+            l, m, first, last = rows[step]
+            if m not in raw_of_row:
+                load_chunk(m, min(M_CHUNK, (l + 1) * (l + 1) - m))
+            x_raw, g_raw, k = raw_of_row[m]
+            g_grouped = side.tile([P, C_OUT, PACK], BF16, align_bytes=64, tag="g_grouped")
+            regroup(nc.scalar.copy, g_grouped[:], g_raw[:, :, k, :])
+            x_grouped = side.tile([P, C_IN, PACK], BF16, align_bytes=64, tag="x_grouped")
+            width = C_IN // pieces_of(step)
+            for c0 in range(0, C_IN, width):
+                regroup(nc.vector.tensor_copy, x_grouped[:, c0 : c0 + width, :], x_raw[:, :, k, c0 : c0 + width])
+            grouped_of_step[step] = (x_grouped, g_grouped)
+
+        def drain(l, acc, t0):
+            staged = staging.tile([P, STORE_TILES, C_OUT], F32, tag="staged")
+            for t in range(STORE_TILES):
+                nc.scalar.activation(out=staged[:, t, :], in_=acc[t0 + t][:], func=COPY, scale=pw[:, l : l + 1])
+            nc.scalar.dma_start(
+                out=out[l].rearrange("(t p) j -> p t j", p=P)[:, t0 : t0 + STORE_TILES, :], in_=staged[:]
+            )
+
+        def multiply_step(step):
+            l, m, first, last = rows[step]
+            x_grouped, g_grouped = grouped_of_step[step]
+            if first:
+                acc_of_degree[l] = [banks.tile([P, C_OUT], F32, name="acc%d" % t, tag="acc") for t in range(IN_TILES)]
+            acc = acc_of_degree[l]
+            g_codes = packed.tile([P, C_OUT], U32, align_bytes=64, tag="g_codes")
+            g_scales = packed.tile([P, C_OUT], U8, align_bytes=64, tag="g_scales")
+            nc.vector.quantize_mx(
+                out=g_codes[:].bitcast(E5M2_X4), scales=g_scales[:], in_=g_grouped[:].rearrange("p c j -> p (c j)")
+            )
+            x_codes = packed.tile([P, C_IN], U32, align_bytes=64, tag="x_codes")
+            x_scales = packed.tile([P, C_IN], U8, align_bytes=64, tag="x_scales")
+            width = C_IN // pieces_of(step)
+            for c0 in range(0, C_IN, width):
+                nc.vector.quantize_mx(
+                    out=x_codes[:, c0 : c0 + width].bitcast(E4M3_X4),
+                    scales=x_scales[:, c0 : c0 + width],
+                    in_=x_grouped[:, c0 : c0 + width, :].rearrange("p c j -> p (c j)"),
+                )
+            for t in range(IN_TILES):
+                nc.tensor.matmul_mx(
+                    out=acc[t][:],
+                    lhsT=x_codes[:, t * P : (t + 1) * P].bitcast(E4M3_X4),
+                    lhsT_scale=x_scales[:, t * P : (t + 1) * P],
+                    rhs=g_codes[:].bitcast(E5M2_X4),
+                    rhs_scale=g_scales[:],
+                    start=first,
+                    stop=last,
+                )
+                if last and (t + 1) % STORE_TILES == 0:
+                    drain(l, acc, t + 1 - STORE_TILES)
+
+        regroup_step(0)
+        for step in range(len(rows)):
+            if step < last_step:
+                regroup_step(step + 1)
+            multiply_step(step)

@@ -22,6 +22,7 @@ RUN = 4
 M_CHUNK = 3
 RAW_BUFS = 4
 STORE_TILES = 2
+G_LEAD = 2
 LAST_PIECES = 4
 
 FLOPS = 2 * NODES * DEGREES * DEGREES * C_IN * C_OUT
@@ -40,52 +41,42 @@ def tile_linear_pa_kernel(tc, x, weights, path_weights, grad_out, out):
     x_nodes = x.rearrange("(p j) m c -> p j m c", j=PACK)
     g_nodes = grad_out.rearrange("(p j) m c -> p j m c", j=PACK)
 
-    rows = []
-    for l in range(DEGREES):
-        for m in range(l * l, (l + 1) * (l + 1)):
-            rows.append((l, m, m == l * l, m == (l + 1) * (l + 1) - 1))
-    last_step = len(rows) - 1
+    degree_of_row = [l for l in range(DEGREES) for m in range(l * l, (l + 1) * (l + 1))]
+    order = list(reversed(range(len(degree_of_row))))
 
     with ExitStack() as ctx:
         consts = ctx.enter_context(tc.tile_pool(name="consts", bufs=1))
         raw = ctx.enter_context(tc.tile_pool(name="raw", bufs=RAW_BUFS))
-        side = ctx.enter_context(tc.tile_pool(name="side", bufs=3))
+        side = ctx.enter_context(tc.tile_pool(name="side", bufs=2))
         packed = ctx.enter_context(tc.tile_pool(name="packed", bufs=3))
         staging = ctx.enter_context(tc.tile_pool(name="staging", bufs=4))
         banks = ctx.enter_context(tc.psum_pool(name="banks", bufs=IN_TILES))
-
         pw_bf16 = consts.tile([P, DEGREES], BF16)
         nc.scalar.dma_start(out=pw_bf16[:], in_=path_weights.partition_broadcast(P))
         pw = consts.tile([P, DEGREES], F32)
-        nc.vector.tensor_copy(out=pw[:], in_=pw_bf16[:])
 
         raw_of_row = {}
-        grouped_of_step = {}
+        g_grouped_of_row = {}
         acc_of_degree = {}
 
-        def load_chunk(m_first, count):
-            x_raw = raw.tile([P, PACK, count, C_IN], BF16, tag="x_raw")
-            nc.sync.dma_start(out=x_raw[:], in_=x_nodes[:, :, m_first : m_first + count, :])
-            g_raw = raw.tile([P, PACK, count, C_OUT], BF16, tag="g_raw")
-            nc.sync.dma_start(out=g_raw[:], in_=g_nodes[:, :, m_first : m_first + count, :])
-            for k in range(count):
-                raw_of_row[m_first + k] = (x_raw, g_raw, k)
-
-        def pieces_of(step):
-            return LAST_PIECES if step == last_step else 1
-
-        def regroup_step(step):
-            l, m, first, last = rows[step]
+        def raw_rows(m):
             if m not in raw_of_row:
-                load_chunk(m, min(M_CHUNK, (l + 1) * (l + 1) - m))
-            x_raw, g_raw, k = raw_of_row[m]
-            g_grouped = side.tile([P, C_OUT, PACK], BF16, align_bytes=64, tag="g_grouped")
+                l = degree_of_row[m]
+                m_low = m - (m - l * l) % M_CHUNK
+                count = m - m_low + 1
+                x_raw = raw.tile([P, PACK, count, C_IN], BF16, tag="x_raw")
+                nc.sync.dma_start(out=x_raw[:], in_=x_nodes[:, :, m_low : m + 1, :])
+                g_raw = raw.tile([P, PACK, count, C_OUT], BF16, tag="g_raw")
+                nc.sync.dma_start(out=g_raw[:], in_=g_nodes[:, :, m_low : m + 1, :])
+                for k in range(count):
+                    raw_of_row[m_low + k] = (x_raw, g_raw, k)
+            return raw_of_row[m]
+
+        def regroup_g(m):
+            x_raw, g_raw, k = raw_rows(m)
+            g_grouped = side.tile([P, C_OUT, PACK], BF16, align_bytes=64, tag="g_grouped", bufs=G_LEAD + 2)
             regroup(nc.scalar.copy, g_grouped[:], g_raw[:, :, k, :])
-            x_grouped = side.tile([P, C_IN, PACK], BF16, align_bytes=64, tag="x_grouped")
-            width = C_IN // pieces_of(step)
-            for c0 in range(0, C_IN, width):
-                regroup(nc.vector.tensor_copy, x_grouped[:, c0 : c0 + width, :], x_raw[:, :, k, c0 : c0 + width])
-            grouped_of_step[step] = (x_grouped, g_grouped)
+            g_grouped_of_row[m] = g_grouped
 
         def drain(l, acc, t0):
             staged = staging.tile([P, STORE_TILES, C_OUT], F32, tag="staged")
@@ -95,41 +86,56 @@ def tile_linear_pa_kernel(tc, x, weights, path_weights, grad_out, out):
                 out=out[l].rearrange("(t p) j -> p t j", p=P)[:, t0 : t0 + STORE_TILES, :], in_=staged[:]
             )
 
-        def multiply_step(step):
-            l, m, first, last = rows[step]
-            x_grouped, g_grouped = grouped_of_step[step]
+        def work_row(m, pieces):
+            l = degree_of_row[m]
+            first = m == (l + 1) * (l + 1) - 1
+            last = m == l * l
+            width = C_IN // pieces
+            x_raw, g_raw, k = raw_rows(m)
+            x_grouped = side.tile([P, C_IN, PACK], BF16, align_bytes=64, tag="x_grouped")
+            x_codes = packed.tile([P, C_IN], U32, align_bytes=64, tag="x_codes")
+            x_scales = packed.tile([P, C_IN], U8, align_bytes=64, tag="x_scales")
+            g_codes = packed.tile([P, C_OUT], U32, align_bytes=64, tag="g_codes")
+            g_scales = packed.tile([P, C_OUT], U8, align_bytes=64, tag="g_scales")
             if first:
                 acc_of_degree[l] = [banks.tile([P, C_OUT], F32, name="acc%d" % t, tag="acc") for t in range(IN_TILES)]
             acc = acc_of_degree[l]
-            g_codes = packed.tile([P, C_OUT], U32, align_bytes=64, tag="g_codes")
-            g_scales = packed.tile([P, C_OUT], U8, align_bytes=64, tag="g_scales")
+
+            def regroup_x(c0):
+                regroup(nc.vector.tensor_copy, x_grouped[:, c0 : c0 + width, :], x_raw[:, :, k, c0 : c0 + width])
+
+            regroup_x(0)
             nc.vector.quantize_mx(
-                out=g_codes[:].bitcast(E5M2_X4), scales=g_scales[:], in_=g_grouped[:].rearrange("p c j -> p (c j)")
+                out=g_codes[:].bitcast(E5M2_X4),
+                scales=g_scales[:],
+                in_=g_grouped_of_row[m][:].rearrange("p c j -> p (c j)"),
             )
-            x_codes = packed.tile([P, C_IN], U32, align_bytes=64, tag="x_codes")
-            x_scales = packed.tile([P, C_IN], U8, align_bytes=64, tag="x_scales")
-            width = C_IN // pieces_of(step)
             for c0 in range(0, C_IN, width):
+                if c0 + width < C_IN:
+                    regroup_x(c0 + width)
                 nc.vector.quantize_mx(
                     out=x_codes[:, c0 : c0 + width].bitcast(E4M3_X4),
                     scales=x_scales[:, c0 : c0 + width],
                     in_=x_grouped[:, c0 : c0 + width, :].rearrange("p c j -> p (c j)"),
                 )
-            for t in range(IN_TILES):
-                nc.tensor.matmul_mx(
-                    out=acc[t][:],
-                    lhsT=x_codes[:, t * P : (t + 1) * P].bitcast(E4M3_X4),
-                    lhsT_scale=x_scales[:, t * P : (t + 1) * P],
-                    rhs=g_codes[:].bitcast(E5M2_X4),
-                    rhs_scale=g_scales[:],
-                    start=first,
-                    stop=last,
-                )
-                if last and (t + 1) % STORE_TILES == 0:
-                    drain(l, acc, t + 1 - STORE_TILES)
+                for t in range(c0 // P, (c0 + width) // P):
+                    nc.tensor.matmul_mx(
+                        out=acc[t][:],
+                        lhsT=x_codes[:, t * P : (t + 1) * P].bitcast(E4M3_X4),
+                        lhsT_scale=x_scales[:, t * P : (t + 1) * P],
+                        rhs=g_codes[:].bitcast(E5M2_X4),
+                        rhs_scale=g_scales[:],
+                        start=first,
+                        stop=last,
+                    )
+                    if last and (t + 1) % STORE_TILES == 0:
+                        drain(l, acc, t + 1 - STORE_TILES)
 
-        regroup_step(0)
-        for step in range(len(rows)):
-            if step < last_step:
-                regroup_step(step + 1)
-            multiply_step(step)
+        for step in range(G_LEAD):
+            regroup_g(order[step])
+        for step in range(len(order)):
+            if step + G_LEAD < len(order):
+                regroup_g(order[step + G_LEAD])
+            work_row(order[step], LAST_PIECES if step == len(order) - 1 else 1)
+            if step == 0:
+                nc.vector.tensor_copy(out=pw[:], in_=pw_bf16[:])

@@ -51,6 +51,7 @@ def tile_linear_pa_kernel(tc, x, weights, path_weights, grad_out, out):
         packed = ctx.enter_context(tc.tile_pool(name="packed", bufs=3))
         staging = ctx.enter_context(tc.tile_pool(name="staging", bufs=4))
         banks = ctx.enter_context(tc.psum_pool(name="banks", bufs=IN_TILES))
+        ctx.enter_context(tc.manual_schedule())
         pw_bf16 = consts.tile([P, DEGREES], BF16)
         nc.scalar.dma_start(out=pw_bf16[:], in_=path_weights.partition_broadcast(P))
         pw = consts.tile([P, DEGREES], F32)

@@ -19,10 +19,11 @@ C_OUT = 512
 IN_TILES = C_IN // P
 RUN = 4
 
+DEGREE_ORDER = (3, 2, 0, 1)
 M_CHUNK = 3
 RAW_BUFS = 4
 STORE_TILES = 2
-G_LEAD = 2
+G_LEAD = 4
 LAST_PIECES = 4
 
 FLOPS = 2 * NODES * DEGREES * DEGREES * C_IN * C_OUT
@@ -42,22 +43,24 @@ def tile_linear_pa_kernel(tc, x, weights, path_weights, grad_out, out):
     g_nodes = grad_out.rearrange("(p j) m c -> p j m c", j=PACK)
 
     degree_of_row = [l for l in range(DEGREES) for m in range(l * l, (l + 1) * (l + 1))]
-    order = list(reversed(range(len(degree_of_row))))
+    order = [m for l in DEGREE_ORDER for m in reversed(range(l * l, (l + 1) * (l + 1)))]
+    last_row = order[-1]
 
     with ExitStack() as ctx:
         consts = ctx.enter_context(tc.tile_pool(name="consts", bufs=1))
         raw = ctx.enter_context(tc.tile_pool(name="raw", bufs=RAW_BUFS))
         side = ctx.enter_context(tc.tile_pool(name="side", bufs=2))
         packed = ctx.enter_context(tc.tile_pool(name="packed", bufs=3))
-        staging = ctx.enter_context(tc.tile_pool(name="staging", bufs=4))
+        staging = ctx.enter_context(tc.tile_pool(name="staging", bufs=2 * IN_TILES // STORE_TILES))
         banks = ctx.enter_context(tc.psum_pool(name="banks", bufs=IN_TILES))
-        ctx.enter_context(tc.manual_schedule())
+
         pw_bf16 = consts.tile([P, DEGREES], BF16)
         nc.scalar.dma_start(out=pw_bf16[:], in_=path_weights.partition_broadcast(P))
         pw = consts.tile([P, DEGREES], F32)
 
         raw_of_row = {}
         g_grouped_of_row = {}
+        g_packed_of_row = {}
         acc_of_degree = {}
 
         def raw_rows(m):
@@ -75,29 +78,40 @@ def tile_linear_pa_kernel(tc, x, weights, path_weights, grad_out, out):
 
         def regroup_g(m):
             x_raw, g_raw, k = raw_rows(m)
-            g_grouped = side.tile([P, C_OUT, PACK], BF16, align_bytes=64, tag="g_grouped", bufs=G_LEAD + 2)
+            g_grouped = side.tile([P, C_OUT, PACK], BF16, align_bytes=64, tag="g_grouped")
             regroup(nc.scalar.copy, g_grouped[:], g_raw[:, :, k, :])
             g_grouped_of_row[m] = g_grouped
+
+        def quantise_g(m):
+            g_codes = packed.tile([P, C_OUT], U32, align_bytes=64, tag="g_codes", bufs=G_LEAD + 2)
+            g_scales = packed.tile([P, C_OUT], U8, align_bytes=64, tag="g_scales", bufs=G_LEAD + 2)
+            nc.vector.quantize_mx(
+                out=g_codes[:].bitcast(E5M2_X4),
+                scales=g_scales[:],
+                in_=g_grouped_of_row[m][:].rearrange("p c j -> p (c j)"),
+            )
+            g_packed_of_row[m] = (g_codes, g_scales)
 
         def drain(l, acc, t0):
             staged = staging.tile([P, STORE_TILES, C_OUT], F32, tag="staged")
             for t in range(STORE_TILES):
-                nc.scalar.activation(out=staged[:, t, :], in_=acc[t0 + t][:], func=COPY, scale=pw[:, l : l + 1])
-            nc.scalar.dma_start(
+                if l == degree_of_row[last_row] and t % 2 == 1:
+                    nc.vector.tensor_scalar_mul(out=staged[:, t, :], in0=acc[t0 + t][:], scalar1=pw[:, l : l + 1])
+                else:
+                    nc.scalar.activation(out=staged[:, t, :], in_=acc[t0 + t][:], func=COPY, scale=pw[:, l : l + 1])
+            nc.sync.dma_start(
                 out=out[l].rearrange("(t p) j -> p t j", p=P)[:, t0 : t0 + STORE_TILES, :], in_=staged[:]
             )
 
-        def work_row(m, pieces):
+        def work_row(m, g_rows_to_quantise):
             l = degree_of_row[m]
             first = m == (l + 1) * (l + 1) - 1
             last = m == l * l
-            width = C_IN // pieces
+            width = C_IN // LAST_PIECES if m == last_row else C_IN
             x_raw, g_raw, k = raw_rows(m)
             x_grouped = side.tile([P, C_IN, PACK], BF16, align_bytes=64, tag="x_grouped")
             x_codes = packed.tile([P, C_IN], U32, align_bytes=64, tag="x_codes")
             x_scales = packed.tile([P, C_IN], U8, align_bytes=64, tag="x_scales")
-            g_codes = packed.tile([P, C_OUT], U32, align_bytes=64, tag="g_codes")
-            g_scales = packed.tile([P, C_OUT], U8, align_bytes=64, tag="g_scales")
             if first:
                 acc_of_degree[l] = [banks.tile([P, C_OUT], F32, name="acc%d" % t, tag="acc") for t in range(IN_TILES)]
             acc = acc_of_degree[l]
@@ -106,11 +120,9 @@ def tile_linear_pa_kernel(tc, x, weights, path_weights, grad_out, out):
                 regroup(nc.vector.tensor_copy, x_grouped[:, c0 : c0 + width, :], x_raw[:, :, k, c0 : c0 + width])
 
             regroup_x(0)
-            nc.vector.quantize_mx(
-                out=g_codes[:].bitcast(E5M2_X4),
-                scales=g_scales[:],
-                in_=g_grouped_of_row[m][:].rearrange("p c j -> p (c j)"),
-            )
+            for g_row in g_rows_to_quantise:
+                quantise_g(g_row)
+            g_codes, g_scales = g_packed_of_row[m]
             for c0 in range(0, C_IN, width):
                 if c0 + width < C_IN:
                     regroup_x(c0 + width)
@@ -137,6 +149,7 @@ def tile_linear_pa_kernel(tc, x, weights, path_weights, grad_out, out):
         for step in range(len(order)):
             if step + G_LEAD < len(order):
                 regroup_g(order[step + G_LEAD])
-            work_row(order[step], LAST_PIECES if step == len(order) - 1 else 1)
+            first_g = 0 if step == 0 else step + G_LEAD - 1
+            work_row(order[step], order[first_g : step + G_LEAD])
             if step == 0:
                 nc.vector.tensor_copy(out=pw[:], in_=pw_bf16[:])

@@ -20,10 +20,12 @@ IN_TILES = C_IN // P
 RUN = 4
 
 DEGREE_ORDER = (3, 2, 0, 1)
-M_CHUNK = 3
-RAW_BUFS = 4
+M_CHUNK = 2
+RAW_BUFS = 6
 STORE_TILES = 2
 G_LEAD = 4
+X_LEAD = 1
+X_SCALAR = 192
 LAST_PIECES = 4
 
 FLOPS = 2 * NODES * DEGREES * DEGREES * C_IN * C_OUT
@@ -59,6 +61,7 @@ def tile_linear_pa_kernel(tc, x, weights, path_weights, grad_out, out):
         pw = consts.tile([P, DEGREES], F32)
 
         raw_of_row = {}
+        x_grouped_of_row = {}
         g_grouped_of_row = {}
         g_packed_of_row = {}
         acc_of_degree = {}
@@ -81,6 +84,17 @@ def tile_linear_pa_kernel(tc, x, weights, path_weights, grad_out, out):
             g_grouped = side.tile([P, C_OUT, PACK], BF16, align_bytes=64, tag="g_grouped")
             regroup(nc.scalar.copy, g_grouped[:], g_raw[:, :, k, :])
             g_grouped_of_row[m] = g_grouped
+
+        def scalar_share(m):
+            return X_SCALAR if degree_of_row[m] in DEGREE_ORDER[:2] else 0
+
+        def start_x(m):
+            x_raw, g_raw, k = raw_rows(m)
+            x_grouped = side.tile([P, C_IN, PACK], BF16, align_bytes=64, tag="x_grouped", bufs=X_LEAD + 1)
+            c0 = C_IN - scalar_share(m)
+            if c0 < C_IN:
+                regroup(nc.scalar.copy, x_grouped[:, c0:, :], x_raw[:, :, k, c0:])
+            x_grouped_of_row[m] = x_grouped
 
         def quantise_g(m):
             g_codes = packed.tile([P, C_OUT], U32, align_bytes=64, tag="g_codes", bufs=G_LEAD + 2)
@@ -109,7 +123,7 @@ def tile_linear_pa_kernel(tc, x, weights, path_weights, grad_out, out):
             last = m == l * l
             width = C_IN // LAST_PIECES if m == last_row else C_IN
             x_raw, g_raw, k = raw_rows(m)
-            x_grouped = side.tile([P, C_IN, PACK], BF16, align_bytes=64, tag="x_grouped")
+            x_grouped = x_grouped_of_row[m]
             x_codes = packed.tile([P, C_IN], U32, align_bytes=64, tag="x_codes")
             x_scales = packed.tile([P, C_IN], U8, align_bytes=64, tag="x_scales")
             if first:
@@ -117,7 +131,8 @@ def tile_linear_pa_kernel(tc, x, weights, path_weights, grad_out, out):
             acc = acc_of_degree[l]
 
             def regroup_x(c0):
-                regroup(nc.vector.tensor_copy, x_grouped[:, c0 : c0 + width, :], x_raw[:, :, k, c0 : c0 + width])
+                c1 = c0 + width - scalar_share(m)
+                regroup(nc.vector.tensor_copy, x_grouped[:, c0:c1, :], x_raw[:, :, k, c0:c1])
 
             regroup_x(0)
             for g_row in g_rows_to_quantise:
@@ -146,7 +161,11 @@ def tile_linear_pa_kernel(tc, x, weights, path_weights, grad_out, out):
 
         for step in range(G_LEAD):
             regroup_g(order[step])
+        for step in range(X_LEAD):
+            start_x(order[step])
         for step in range(len(order)):
+            if step + X_LEAD < len(order):
+                start_x(order[step + X_LEAD])
             if step + G_LEAD < len(order):
                 regroup_g(order[step + G_LEAD])
             first_g = 0 if step == 0 else step + G_LEAD - 1

@@ -17,7 +17,7 @@ DEGREES = 4
 C_IN = 1024
 C_OUT = 512
 IN_TILES = C_IN // P
-RUN = 4
+RUN = 8
 
 DEGREE_ORDER = (3, 2, 0, 1)
 M_CHUNK = 2

@@ -17,16 +17,37 @@ DEGREES = 4
 C_IN = 1024
 C_OUT = 512
 IN_TILES = C_IN // P
+PAIR = 2
+PAIR_CHANNELS = PAIR * P
 RUN = 8
 
 DEGREE_ORDER = (3, 2, 0, 1)
-M_CHUNK = 2
-RAW_BUFS = 6
-STORE_TILES = 2
-G_LEAD = 4
-X_LEAD = 1
-X_SCALAR = 192
-LAST_PIECES = 4
+LOADS = (
+    ("x", 15, 16),
+    ("g", 15, 16),
+    ("x", 14, 15),
+    ("g", 14, 15),
+    ("x", 13, 14),
+    ("g", 12, 14),
+    ("x", 11, 13),
+    ("g", 10, 12),
+    ("x", 9, 11),
+    ("g", 8, 10),
+    ("x", 7, 9),
+    ("g", 4, 8),
+    ("x", 5, 7),
+    ("x", 4, 5),
+    ("g", 0, 4),
+    ("x", 0, 1),
+    ("x", 2, 4),
+    ("x", 1, 2),
+)
+RAW_BUFS = {"x1": 3, "x2": 3, "g1": 2, "g2": 2, "g4": 2}
+LOAD_LEAD = 10
+SCALAR_LEAD = 3
+X_SCALAR = {3: 1, 2: 0, 0: 0, 1: 0}
+VECTOR_TILES = {3: (), 2: (), 0: (), 1: (7,)}
+LAST_GROUP = 256
 
 FLOPS = 2 * NODES * DEGREES * DEGREES * C_IN * C_OUT
 BYTES = 2 * NODES * DEGREES * DEGREES * (C_IN + C_OUT) + 4 * DEGREES * C_IN * C_OUT + 2 * DEGREES
@@ -39,6 +60,16 @@ def regroup(copy, grouped, raw_row):
     )
 
 
+def regroup_pairs(copy, grouped, raw_row, first_tile, last_tile):
+    for t in range(PAIR):
+        pairs = slice((first_tile + PAIR - 1 - t) // PAIR, (last_tile + PAIR - 1 - t) // PAIR)
+        if pairs.start < pairs.stop:
+            copy(
+                out=grouped.rearrange("p (q t b i) j -> p t b q j i", t=PAIR, b=P // RUN, i=RUN)[:, t, :, pairs],
+                in_=raw_row.rearrange("p j (q b i t) -> p t b q j i", t=PAIR, b=P // RUN, i=RUN)[:, t, :, pairs],
+            )
+
+
 def tile_linear_pa_kernel(tc, x, weights, path_weights, grad_out, out):
     nc = tc.nc
     x_nodes = x.rearrange("(p j) m c -> p j m c", j=PACK)
@@ -46,59 +77,68 @@ def tile_linear_pa_kernel(tc, x, weights, path_weights, grad_out, out):
 
     degree_of_row = [l for l in range(DEGREES) for m in range(l * l, (l + 1) * (l + 1))]
     order = [m for l in DEGREE_ORDER for m in reversed(range(l * l, (l + 1) * (l + 1)))]
-    last_row = order[-1]
+    last_degree = DEGREE_ORDER[-1]
+
+    steps = [(m, 0, C_IN) for m in order if degree_of_row[m] != last_degree]
+    steps += [(m, c0, c0 + LAST_GROUP) for c0 in range(0, C_IN, LAST_GROUP) for m in order if degree_of_row[m] == last_degree]
 
     with ExitStack() as ctx:
         consts = ctx.enter_context(tc.tile_pool(name="consts", bufs=1))
-        raw = ctx.enter_context(tc.tile_pool(name="raw", bufs=RAW_BUFS))
+        raw = ctx.enter_context(tc.tile_pool(name="raw", bufs=2))
         side = ctx.enter_context(tc.tile_pool(name="side", bufs=2))
         packed = ctx.enter_context(tc.tile_pool(name="packed", bufs=3))
-        staging = ctx.enter_context(tc.tile_pool(name="staging", bufs=2 * IN_TILES // STORE_TILES))
+        staging = ctx.enter_context(tc.tile_pool(name="staging", bufs=8))
         banks = ctx.enter_context(tc.psum_pool(name="banks", bufs=IN_TILES))
 
         pw_bf16 = consts.tile([P, DEGREES], BF16)
-        nc.scalar.dma_start(out=pw_bf16[:], in_=path_weights.partition_broadcast(P))
         pw = consts.tile([P, DEGREES], F32)
 
-        raw_of_row = {}
-        x_grouped_of_row = {}
+        loads = list(LOADS)
+        raw_of_row = {"x": {}, "g": {}}
         g_grouped_of_row = {}
         g_packed_of_row = {}
-        acc_of_degree = {}
+        x_grouped_of_step = {}
+        acc_of_tile = {}
 
-        def raw_rows(m):
-            if m not in raw_of_row:
-                l = degree_of_row[m]
-                m_low = m - (m - l * l) % M_CHUNK
-                count = m - m_low + 1
-                x_raw = raw.tile([P, PACK, count, C_IN], BF16, tag="x_raw")
-                nc.sync.dma_start(out=x_raw[:], in_=x_nodes[:, :, m_low : m + 1, :])
-                g_raw = raw.tile([P, PACK, count, C_OUT], BF16, tag="g_raw")
-                nc.sync.dma_start(out=g_raw[:], in_=g_nodes[:, :, m_low : m + 1, :])
-                for k in range(count):
-                    raw_of_row[m_low + k] = (x_raw, g_raw, k)
-            return raw_of_row[m]
+        def load(name, low, high):
+            nodes, channels = (x_nodes, C_IN) if name == "x" else (g_nodes, C_OUT)
+            tag = "%s%d" % (name, high - low)
+            rows = raw.tile([P, PACK, high - low, channels], BF16, name="rows", tag=tag, bufs=RAW_BUFS[tag])
+            nc.sync.dma_start(out=rows[:], in_=nodes[:, :, low:high, :])
+            for m in range(low, high):
+                raw_of_row[name][m] = (rows, m - low)
+
+        def load_up_to(row_count):
+            while min(len(raw_of_row["x"]), len(raw_of_row["g"])) < min(row_count, len(order)):
+                load(*loads.pop(0))
 
         def regroup_g(m):
-            x_raw, g_raw, k = raw_rows(m)
-            g_grouped = side.tile([P, C_OUT, PACK], BF16, align_bytes=64, tag="g_grouped")
-            regroup(nc.scalar.copy, g_grouped[:], g_raw[:, :, k, :])
+            rows, k = raw_of_row["g"][m]
+            g_grouped = side.tile([P, C_OUT, PACK], BF16, align_bytes=64, tag="g_grouped", bufs=4)
+            regroup(nc.scalar.copy, g_grouped[:], rows[:, :, k, :])
             g_grouped_of_row[m] = g_grouped
 
-        def scalar_share(m):
-            return X_SCALAR if degree_of_row[m] in DEGREE_ORDER[:2] else 0
+        def scalar_split(i):
+            m, c0, c1 = steps[i]
+            return (c1 - c0) // P - X_SCALAR[degree_of_row[m]]
 
-        def start_x(m):
-            x_raw, g_raw, k = raw_rows(m)
-            x_grouped = side.tile([P, C_IN, PACK], BF16, align_bytes=64, tag="x_grouped", bufs=X_LEAD + 1)
-            c0 = C_IN - scalar_share(m)
-            if c0 < C_IN:
-                regroup(nc.scalar.copy, x_grouped[:, c0:, :], x_raw[:, :, k, c0:])
-            x_grouped_of_row[m] = x_grouped
+        def regroup_x_scalar(i):
+            m, c0, c1 = steps[i]
+            rows, k = raw_of_row["x"][m]
+            x_grouped = side.tile([P, c1 - c0, PACK], BF16, align_bytes=64, tag="x_grouped", bufs=3)
+            split = scalar_split(i)
+            regroup_pairs(nc.scalar.copy, x_grouped[:], rows[:, :, k, c0:c1], split, (c1 - c0) // P)
+            x_grouped_of_step[i] = x_grouped
+
+        def regroup_x_vector(i):
+            m, c0, c1 = steps[i]
+            rows, k = raw_of_row["x"][m]
+            split = scalar_split(i)
+            regroup_pairs(nc.vector.tensor_copy, x_grouped_of_step[i][:], rows[:, :, k, c0:c1], 0, split)
 
         def quantise_g(m):
-            g_codes = packed.tile([P, C_OUT], U32, align_bytes=64, tag="g_codes", bufs=G_LEAD + 2)
-            g_scales = packed.tile([P, C_OUT], U8, align_bytes=64, tag="g_scales", bufs=G_LEAD + 2)
+            g_codes = packed.tile([P, C_OUT], U32, align_bytes=64, tag="g_codes", bufs=6)
+            g_scales = packed.tile([P, C_OUT], U8, align_bytes=64, tag="g_scales", bufs=6)
             nc.vector.quantize_mx(
                 out=g_codes[:].bitcast(E5M2_X4),
                 scales=g_scales[:],
@@ -106,69 +146,83 @@ def tile_linear_pa_kernel(tc, x, weights, path_weights, grad_out, out):
             )
             g_packed_of_row[m] = (g_codes, g_scales)
 
-        def drain(l, acc, t0):
-            staged = staging.tile([P, STORE_TILES, C_OUT], F32, tag="staged")
-            for t in range(STORE_TILES):
-                if l == degree_of_row[last_row] and t % 2 == 1:
-                    nc.vector.tensor_scalar_mul(out=staged[:, t, :], in0=acc[t0 + t][:], scalar1=pw[:, l : l + 1])
-                else:
-                    nc.scalar.activation(out=staged[:, t, :], in_=acc[t0 + t][:], func=COPY, scale=pw[:, l : l + 1])
-            nc.sync.dma_start(
-                out=out[l].rearrange("(t p) j -> p t j", p=P)[:, t0 : t0 + STORE_TILES, :], in_=staged[:]
+        def quantise_x(i):
+            m, c0, c1 = steps[i]
+            x_codes = packed.tile([P, c1 - c0], U32, align_bytes=64, tag="x_codes")
+            x_scales = packed.tile([P, c1 - c0], U8, align_bytes=64, tag="x_scales")
+            nc.vector.quantize_mx(
+                out=x_codes[:].bitcast(E4M3_X4),
+                scales=x_scales[:],
+                in_=x_grouped_of_step[i][:].rearrange("p c j -> p (c j)"),
             )
+            return x_codes, x_scales
 
-        def work_row(m, g_rows_to_quantise):
+        def multiply(i, x_codes, x_scales):
+            m, c0, c1 = steps[i]
             l = degree_of_row[m]
             first = m == (l + 1) * (l + 1) - 1
             last = m == l * l
-            width = C_IN // LAST_PIECES if m == last_row else C_IN
-            x_raw, g_raw, k = raw_rows(m)
-            x_grouped = x_grouped_of_row[m]
-            x_codes = packed.tile([P, C_IN], U32, align_bytes=64, tag="x_codes")
-            x_scales = packed.tile([P, C_IN], U8, align_bytes=64, tag="x_scales")
-            if first:
-                acc_of_degree[l] = [banks.tile([P, C_OUT], F32, name="acc%d" % t, tag="acc") for t in range(IN_TILES)]
-            acc = acc_of_degree[l]
-
-            def regroup_x(c0):
-                c1 = c0 + width - scalar_share(m)
-                regroup(nc.vector.tensor_copy, x_grouped[:, c0:c1, :], x_raw[:, :, k, c0:c1])
-
-            regroup_x(0)
-            for g_row in g_rows_to_quantise:
-                quantise_g(g_row)
             g_codes, g_scales = g_packed_of_row[m]
-            for c0 in range(0, C_IN, width):
-                if c0 + width < C_IN:
-                    regroup_x(c0 + width)
-                nc.vector.quantize_mx(
-                    out=x_codes[:, c0 : c0 + width].bitcast(E4M3_X4),
-                    scales=x_scales[:, c0 : c0 + width],
-                    in_=x_grouped[:, c0 : c0 + width, :].rearrange("p c j -> p (c j)"),
+            for t in range(c0 // P, c1 // P):
+                if first:
+                    acc_of_tile[(l, t)] = banks.tile([P, C_OUT], F32, name="acc%d" % t, tag="acc")
+                columns = slice(t * P - c0, (t + 1) * P - c0)
+                nc.tensor.matmul_mx(
+                    out=acc_of_tile[(l, t)][:],
+                    lhsT=x_codes[:, columns].bitcast(E4M3_X4),
+                    lhsT_scale=x_scales[:, columns],
+                    rhs=g_codes[:].bitcast(E5M2_X4),
+                    rhs_scale=g_scales[:],
+                    start=first,
+                    stop=last,
                 )
-                for t in range(c0 // P, (c0 + width) // P):
-                    nc.tensor.matmul_mx(
-                        out=acc[t][:],
-                        lhsT=x_codes[:, t * P : (t + 1) * P].bitcast(E4M3_X4),
-                        lhsT_scale=x_scales[:, t * P : (t + 1) * P],
-                        rhs=g_codes[:].bitcast(E5M2_X4),
-                        rhs_scale=g_scales[:],
-                        start=first,
-                        stop=last,
-                    )
-                    if last and (t + 1) % STORE_TILES == 0:
-                        drain(l, acc, t + 1 - STORE_TILES)
 
-        for step in range(G_LEAD):
-            regroup_g(order[step])
-        for step in range(X_LEAD):
-            start_x(order[step])
-        for step in range(len(order)):
-            if step + X_LEAD < len(order):
-                start_x(order[step + X_LEAD])
-            if step + G_LEAD < len(order):
-                regroup_g(order[step + G_LEAD])
-            first_g = 0 if step == 0 else step + G_LEAD - 1
-            work_row(order[step], order[first_g : step + G_LEAD])
-            if step == 0:
-                nc.vector.tensor_copy(out=pw[:], in_=pw_bf16[:])
+        def drain(l, t0):
+            staged = staging.tile([P, PAIR, C_OUT], F32, tag="staged")
+            for t in range(t0, t0 + PAIR):
+                acc = acc_of_tile[(l, t)]
+                if t in VECTOR_TILES[l]:
+                    nc.vector.tensor_scalar_mul(out=staged[:, t - t0, :], in0=acc[:], scalar1=pw[:, l : l + 1])
+                else:
+                    nc.scalar.activation(out=staged[:, t - t0, :], in_=acc[:], func=COPY, scale=pw[:, l : l + 1])
+            nc.sync.dma_start(
+                out=out[l].rearrange("(q p t) j -> p q t j", p=P, t=PAIR)[:, t0 // PAIR], in_=staged[:]
+            )
+
+        ctx.enter_context(tc.manual_schedule())
+
+        scalar_done = 0
+        vector_done = 0
+        finished = []
+
+        load_up_to(2)
+        nc.sync.dma_start(out=pw_bf16[:], in_=path_weights.partition_broadcast(P))
+        load_up_to(4)
+        for i, (m, c0, c1) in enumerate(steps):
+            load_up_to(i + 1 + LOAD_LEAD)
+            while scalar_done < min(i + 1 + SCALAR_LEAD, len(steps)):
+                regroup_x_scalar(scalar_done)
+                if scalar_done < len(order):
+                    regroup_g(order[scalar_done])
+                scalar_done += 1
+
+            if i == 3:
+                nc.scalar.copy(out=pw[:], in_=pw_bf16[:])
+            if i == 0:
+                regroup_x_vector(0)
+                x_packed = quantise_x(0)
+            if i + 1 < len(steps):
+                regroup_x_vector(i + 1)
+            if i < len(order):
+                quantise_g(order[i])
+            if i > 0:
+                x_packed = quantise_x(i)
+            multiply(i, *x_packed)
+            for pair in finished:
+                drain(*pair)
+            finished = []
+            if m == degree_of_row[m] ** 2:
+                finished += [(degree_of_row[m], t) for t in range(c0 // P, c1 // P, PAIR)]
+
+        for pair in finished:
+            drain(*pair)

@@ -21,30 +21,30 @@ PAIR = 2
 PAIR_CHANNELS = PAIR * P
 RUN = 8
 
-DEGREE_ORDER = (3, 2, 0, 1)
+DEGREE_ORDER = (0, 3, 2, 1)
 LOADS = (
+    ("x", 0, 1),
+    ("g", 0, 1),
     ("x", 15, 16),
-    ("g", 15, 16),
+    ("g", 14, 16),
     ("x", 14, 15),
-    ("g", 14, 15),
     ("x", 13, 14),
     ("g", 12, 14),
-    ("x", 11, 13),
-    ("g", 10, 12),
-    ("x", 9, 11),
-    ("g", 8, 10),
-    ("x", 7, 9),
-    ("g", 4, 8),
-    ("x", 5, 7),
-    ("x", 4, 5),
-    ("g", 0, 4),
-    ("x", 0, 1),
+    ("x", 12, 13),
+    ("x", 10, 12),
+    ("g", 9, 12),
+    ("x", 8, 10),
+    ("g", 6, 9),
+    ("x", 6, 8),
+    ("g", 4, 6),
+    ("x", 4, 6),
+    ("g", 1, 4),
     ("x", 2, 4),
     ("x", 1, 2),
 )
-RAW_BUFS = {"x1": 3, "x2": 3, "g1": 2, "g2": 2, "g4": 2}
-LOAD_LEAD = 10
-SCALAR_LEAD = 3
+RAW_BUFS = {"x1": 3, "x2": 3, "g1": 1, "g2": 2, "g3": 2}
+LOAD_LEAD = 16
+SCALAR_LEAD = 2
 X_SCALAR = {3: 1, 2: 0, 0: 0, 1: 0}
 VECTOR_TILES = {3: (), 2: (), 0: (), 1: (7,)}
 LAST_GROUP = 256
@@ -114,7 +114,7 @@ def tile_linear_pa_kernel(tc, x, weights, path_weights, grad_out, out):
 
         def regroup_g(m):
             rows, k = raw_of_row["g"][m]
-            g_grouped = side.tile([P, C_OUT, PACK], BF16, align_bytes=64, tag="g_grouped", bufs=4)
+            g_grouped = side.tile([P, C_OUT, PACK], BF16, align_bytes=64, tag="g_grouped", bufs=3)
             regroup(nc.scalar.copy, g_grouped[:], rows[:, :, k, :])
             g_grouped_of_row[m] = g_grouped
 
@@ -206,7 +206,7 @@ def tile_linear_pa_kernel(tc, x, weights, path_weights, grad_out, out):
                     regroup_g(order[scalar_done])
                 scalar_done += 1
 
-            if i == 3:
+            if i == 0:
                 nc.scalar.copy(out=pw[:], in_=pw_bf16[:])
             if i == 0:
                 regroup_x_vector(0)

@@ -25,29 +25,26 @@ DEGREE_ORDER = (0, 3, 2, 1)
 LOADS = (
     ("x", 0, 1),
     ("g", 0, 1),
-    ("x", 15, 16),
-    ("g", 14, 16),
-    ("x", 14, 15),
-    ("x", 13, 14),
-    ("g", 12, 14),
-    ("x", 12, 13),
+    ("x", 14, 16),
+    ("g", 13, 16),
+    ("x", 12, 14),
+    ("g", 10, 13),
     ("x", 10, 12),
-    ("g", 9, 12),
     ("x", 8, 10),
-    ("g", 6, 9),
+    ("g", 7, 10),
     ("x", 6, 8),
-    ("g", 4, 6),
+    ("g", 4, 7),
     ("x", 4, 6),
-    ("g", 1, 4),
     ("x", 2, 4),
+    ("g", 1, 4),
     ("x", 1, 2),
 )
-RAW_BUFS = {"x1": 3, "x2": 3, "g1": 1, "g2": 2, "g3": 2}
+RAW_BUFS = {"x1": 1, "x2": 4, "g1": 1, "g3": 2}
 LOAD_LEAD = 16
 SCALAR_LEAD = 2
 X_SCALAR = {3: 1, 2: 0, 0: 0, 1: 0}
 VECTOR_TILES = {3: (), 2: (), 0: (), 1: (7,)}
-LAST_GROUP = 256
+LAST_GROUPS = ((0, 512), (512, 768), (768, 1024))
 
 FLOPS = 2 * NODES * DEGREES * DEGREES * C_IN * C_OUT
 BYTES = 2 * NODES * DEGREES * DEGREES * (C_IN + C_OUT) + 4 * DEGREES * C_IN * C_OUT + 2 * DEGREES
@@ -80,7 +77,7 @@ def tile_linear_pa_kernel(tc, x, weights, path_weights, grad_out, out):
     last_degree = DEGREE_ORDER[-1]
 
     steps = [(m, 0, C_IN) for m in order if degree_of_row[m] != last_degree]
-    steps += [(m, c0, c0 + LAST_GROUP) for c0 in range(0, C_IN, LAST_GROUP) for m in order if degree_of_row[m] == last_degree]
+    steps += [(m, c0, c1) for c0, c1 in LAST_GROUPS for m in order if degree_of_row[m] == last_degree]
 
     with ExitStack() as ctx:
         consts = ctx.enter_context(tc.tile_pool(name="consts", bufs=1))
@@ -213,10 +210,10 @@ def tile_linear_pa_kernel(tc, x, weights, path_weights, grad_out, out):
                 x_packed = quantise_x(0)
             if i + 1 < len(steps):
                 regroup_x_vector(i + 1)
-            if i < len(order):
-                quantise_g(order[i])
             if i > 0:
                 x_packed = quantise_x(i)
+            if i < len(order):
+                quantise_g(order[i])
             multiply(i, *x_packed)
             for pair in finished:
                 drain(*pair)

@@ -17,8 +17,7 @@ DEGREES = 4
 C_IN = 1024
 C_OUT = 512
 IN_TILES = C_IN // P
-PAIR = 2
-PAIR_CHANNELS = PAIR * P
+STORE_TILES = {0: 4, 3: 4, 2: 2, 1: 2}
 RUN = 8
 
 DEGREE_ORDER = (0, 3, 2, 1)
@@ -39,10 +38,11 @@ LOADS = (
     ("g", 1, 4),
     ("x", 1, 2),
 )
-RAW_BUFS = {"x1": 1, "x2": 4, "g1": 1, "g3": 2}
+RAW_BUFS = {"x1": 1, "g1": 1, "x2": 4, "g3": 2}
 LOAD_LEAD = 16
+STAGED_BUFS = {4: 4, 2: 5}
 SCALAR_LEAD = 2
-X_SCALAR = {3: 1, 2: 0, 0: 0, 1: 0}
+X_SCALAR = {3: 1, 2: 1, 0: 0, 1: 0}
 VECTOR_TILES = {3: (), 2: (), 0: (), 1: (7,)}
 LAST_GROUPS = ((0, 512), (512, 768), (768, 1024))
 
@@ -57,13 +57,13 @@ def regroup(copy, grouped, raw_row):
     )
 
 
-def regroup_pairs(copy, grouped, raw_row, first_tile, last_tile):
-    for t in range(PAIR):
-        pairs = slice((first_tile + PAIR - 1 - t) // PAIR, (last_tile + PAIR - 1 - t) // PAIR)
-        if pairs.start < pairs.stop:
+def regroup_tiles(copy, grouped, raw_row, n, first_tile, last_tile):
+    for t in range(n):
+        blocks = slice((first_tile + n - 1 - t) // n, (last_tile + n - 1 - t) // n)
+        if blocks.start < blocks.stop:
             copy(
-                out=grouped.rearrange("p (q t b i) j -> p t b q j i", t=PAIR, b=P // RUN, i=RUN)[:, t, :, pairs],
-                in_=raw_row.rearrange("p j (q b i t) -> p t b q j i", t=PAIR, b=P // RUN, i=RUN)[:, t, :, pairs],
+                out=grouped.rearrange("p (q t b i) j -> p t b q j i", t=n, b=P // RUN, i=RUN)[:, t, :, blocks],
+                in_=raw_row.rearrange("p j (q b i t) -> p t b q j i", t=n, b=P // RUN, i=RUN)[:, t, :, blocks],
             )
 
 
@@ -124,18 +124,18 @@ def tile_linear_pa_kernel(tc, x, weights, path_weights, grad_out, out):
             rows, k = raw_of_row["x"][m]
             x_grouped = side.tile([P, c1 - c0, PACK], BF16, align_bytes=64, tag="x_grouped", bufs=3)
             split = scalar_split(i)
-            regroup_pairs(nc.scalar.copy, x_grouped[:], rows[:, :, k, c0:c1], split, (c1 - c0) // P)
+            regroup_tiles(nc.scalar.copy, x_grouped[:], rows[:, :, k, c0:c1], STORE_TILES[degree_of_row[m]], split, (c1 - c0) // P)
             x_grouped_of_step[i] = x_grouped
 
         def regroup_x_vector(i):
             m, c0, c1 = steps[i]
             rows, k = raw_of_row["x"][m]
             split = scalar_split(i)
-            regroup_pairs(nc.vector.tensor_copy, x_grouped_of_step[i][:], rows[:, :, k, c0:c1], 0, split)
+            regroup_tiles(nc.vector.tensor_copy, x_grouped_of_step[i][:], rows[:, :, k, c0:c1], STORE_TILES[degree_of_row[m]], 0, split)
 
         def quantise_g(m):
-            g_codes = packed.tile([P, C_OUT], U32, align_bytes=64, tag="g_codes", bufs=6)
-            g_scales = packed.tile([P, C_OUT], U8, align_bytes=64, tag="g_scales", bufs=6)
+            g_codes = packed.tile([P, C_OUT], U32, align_bytes=64, tag="g_codes", bufs=5)
+            g_scales = packed.tile([P, C_OUT], U8, align_bytes=64, tag="g_scales", bufs=5)
             nc.vector.quantize_mx(
                 out=g_codes[:].bitcast(E5M2_X4),
                 scales=g_scales[:],
@@ -175,16 +175,15 @@ def tile_linear_pa_kernel(tc, x, weights, path_weights, grad_out, out):
                 )
 
         def drain(l, t0):
-            staged = staging.tile([P, PAIR, C_OUT], F32, tag="staged")
-            for t in range(t0, t0 + PAIR):
-                acc = acc_of_tile[(l, t)]
-                if t in VECTOR_TILES[l]:
-                    nc.vector.tensor_scalar_mul(out=staged[:, t - t0, :], in0=acc[:], scalar1=pw[:, l : l + 1])
+            n = STORE_TILES[l]
+            staged = staging.tile([P, n, C_OUT], F32, tag="staged%d" % n, bufs=STAGED_BUFS[n])
+            for t in range(n):
+                acc = acc_of_tile[(l, t0 + t)]
+                if t0 + t in VECTOR_TILES[l]:
+                    nc.vector.tensor_scalar_mul(out=staged[:, t, :], in0=acc[:], scalar1=pw[:, l : l + 1])
                 else:
-                    nc.scalar.activation(out=staged[:, t - t0, :], in_=acc[:], func=COPY, scale=pw[:, l : l + 1])
-            nc.sync.dma_start(
-                out=out[l].rearrange("(q p t) j -> p q t j", p=P, t=PAIR)[:, t0 // PAIR], in_=staged[:]
-            )
+                    nc.scalar.activation(out=staged[:, t, :], in_=acc[:], func=COPY, scale=pw[:, l : l + 1])
+            nc.sync.dma_start(out=out[l].rearrange("(q p t) j -> p q t j", p=P, t=n)[:, t0 // n], in_=staged[:])
 
         ctx.enter_context(tc.manual_schedule())
 
@@ -219,7 +218,7 @@ def tile_linear_pa_kernel(tc, x, weights, path_weights, grad_out, out):
                 drain(*pair)
             finished = []
             if m == degree_of_row[m] ** 2:
-                finished += [(degree_of_row[m], t) for t in range(c0 // P, c1 // P, PAIR)]
+                finished += [(degree_of_row[m], t) for t in range(c0 // P, c1 // P, STORE_TILES[degree_of_row[m]])]
 
         for pair in finished:
             drain(*pair)

from contextlib import ExitStack

import concourse.mybir as mybir

BF16 = mybir.dt.bfloat16
F32 = mybir.dt.float32
U32 = mybir.dt.uint32
U8 = mybir.dt.uint8
E4M3_X4 = mybir.dt.float8_e4m3fn_x4
E5M2_X4 = mybir.dt.float8_e5m2_x4
COPY = mybir.ActivationFunctionType.Copy

P = 128
PACK = 4
NODES = P * PACK
DEGREES = 4
C_IN = 1024
C_OUT = 512
IN_TILES = C_IN // P
STORE_TILES = {0: 4, 3: 4, 2: 2, 1: 2}
RUN = 8

DEGREE_ORDER = (0, 3, 2, 1)
LOADS = (
    ("x", 0, 1),
    ("g", 0, 1),
    ("x", 14, 16),
    ("g", 13, 16),
    ("x", 12, 14),
    ("g", 10, 13),
    ("x", 10, 12),
    ("x", 8, 10),
    ("g", 7, 10),
    ("x", 6, 8),
    ("g", 4, 7),
    ("x", 4, 6),
    ("x", 2, 4),
    ("g", 1, 4),
    ("x", 1, 2),
)
RAW_BUFS = {"x1": 1, "g1": 1, "x2": 4, "g3": 2}
LOAD_LEAD = 16
STAGED_BUFS = {4: 4, 2: 5}
SCALAR_LEAD = 2
X_SCALAR = {3: 1, 2: 1, 0: 0, 1: 0}
VECTOR_TILES = {3: (), 2: (), 0: (), 1: (7,)}
LAST_GROUPS = ((0, 512), (512, 768), (768, 1024))

FLOPS = 2 * NODES * DEGREES * DEGREES * C_IN * C_OUT
BYTES = 2 * NODES * DEGREES * DEGREES * (C_IN + C_OUT) + 4 * DEGREES * C_IN * C_OUT + 2 * DEGREES


def regroup(copy, grouped, raw_row):
    copy(
        out=grouped.rearrange("p (c i) j -> p c j i", i=RUN),
        in_=raw_row.rearrange("p j (c i) -> p c j i", i=RUN),
    )


def regroup_tiles(copy, grouped, raw_row, n, first_tile, last_tile):
    for t in range(n):
        blocks = slice((first_tile + n - 1 - t) // n, (last_tile + n - 1 - t) // n)
        if blocks.start < blocks.stop:
            copy(
                out=grouped.rearrange("p (q t b i) j -> p t b q j i", t=n, b=P // RUN, i=RUN)[:, t, :, blocks],
                in_=raw_row.rearrange("p j (q b i t) -> p t b q j i", t=n, b=P // RUN, i=RUN)[:, t, :, blocks],
            )


def tile_linear_pa_kernel(tc, x, weights, path_weights, grad_out, out):
    nc = tc.nc
    x_nodes = x.rearrange("(p j) m c -> p j m c", j=PACK)
    g_nodes = grad_out.rearrange("(p j) m c -> p j m c", j=PACK)

    degree_of_row = [l for l in range(DEGREES) for m in range(l * l, (l + 1) * (l + 1))]
    order = [m for l in DEGREE_ORDER for m in reversed(range(l * l, (l + 1) * (l + 1)))]
    last_degree = DEGREE_ORDER[-1]

    steps = [(m, 0, C_IN) for m in order if degree_of_row[m] != last_degree]
    steps += [(m, c0, c1) for c0, c1 in LAST_GROUPS for m in order if degree_of_row[m] == last_degree]

    with ExitStack() as ctx:
        consts = ctx.enter_context(tc.tile_pool(name="consts", bufs=1))
        raw = ctx.enter_context(tc.tile_pool(name="raw", bufs=2))
        side = ctx.enter_context(tc.tile_pool(name="side", bufs=2))
        packed = ctx.enter_context(tc.tile_pool(name="packed", bufs=3))
        staging = ctx.enter_context(tc.tile_pool(name="staging", bufs=8))
        banks = ctx.enter_context(tc.psum_pool(name="banks", bufs=IN_TILES))

        pw_bf16 = consts.tile([P, DEGREES], BF16)
        pw = consts.tile([P, DEGREES], F32)

        loads = list(LOADS)
        raw_of_row = {"x": {}, "g": {}}
        g_grouped_of_row = {}
        g_packed_of_row = {}
        x_grouped_of_step = {}
        acc_of_tile = {}

        def load(name, low, high):
            nodes, channels = (x_nodes, C_IN) if name == "x" else (g_nodes, C_OUT)
            tag = "%s%d" % (name, high - low)
            rows = raw.tile([P, PACK, high - low, channels], BF16, name="rows", tag=tag, bufs=RAW_BUFS[tag])
            nc.sync.dma_start(out=rows[:], in_=nodes[:, :, low:high, :])
            for m in range(low, high):
                raw_of_row[name][m] = (rows, m - low)

        def load_up_to(row_count):
            while min(len(raw_of_row["x"]), len(raw_of_row["g"])) < min(row_count, len(order)):
                load(*loads.pop(0))

        def regroup_g(m):
            rows, k = raw_of_row["g"][m]
            g_grouped = side.tile([P, C_OUT, PACK], BF16, align_bytes=64, tag="g_grouped", bufs=3)
            regroup(nc.scalar.copy, g_grouped[:], rows[:, :, k, :])
            g_grouped_of_row[m] = g_grouped

        def scalar_split(i):
            m, c0, c1 = steps[i]
            return (c1 - c0) // P - X_SCALAR[degree_of_row[m]]

        def regroup_x_scalar(i):
            m, c0, c1 = steps[i]
            rows, k = raw_of_row["x"][m]
            x_grouped = side.tile([P, c1 - c0, PACK], BF16, align_bytes=64, tag="x_grouped", bufs=3)
            split = scalar_split(i)
            regroup_tiles(nc.scalar.copy, x_grouped[:], rows[:, :, k, c0:c1], STORE_TILES[degree_of_row[m]], split, (c1 - c0) // P)
            x_grouped_of_step[i] = x_grouped

        def regroup_x_vector(i):
            m, c0, c1 = steps[i]
            rows, k = raw_of_row["x"][m]
            split = scalar_split(i)
            regroup_tiles(nc.vector.tensor_copy, x_grouped_of_step[i][:], rows[:, :, k, c0:c1], STORE_TILES[degree_of_row[m]], 0, split)

        def quantise_g(m):
            g_codes = packed.tile([P, C_OUT], U32, align_bytes=64, tag="g_codes", bufs=5)
            g_scales = packed.tile([P, C_OUT], U8, align_bytes=64, tag="g_scales", bufs=5)
            nc.vector.quantize_mx(
                out=g_codes[:].bitcast(E5M2_X4),
                scales=g_scales[:],
                in_=g_grouped_of_row[m][:].rearrange("p c j -> p (c j)"),
            )
            g_packed_of_row[m] = (g_codes, g_scales)

        def quantise_x(i):
            m, c0, c1 = steps[i]
            x_codes = packed.tile([P, c1 - c0], U32, align_bytes=64, tag="x_codes")
            x_scales = packed.tile([P, c1 - c0], U8, align_bytes=64, tag="x_scales")
            nc.vector.quantize_mx(
                out=x_codes[:].bitcast(E4M3_X4),
                scales=x_scales[:],
                in_=x_grouped_of_step[i][:].rearrange("p c j -> p (c j)"),
            )
            return x_codes, x_scales

        def multiply(i, x_codes, x_scales):
            m, c0, c1 = steps[i]
            l = degree_of_row[m]
            first = m == (l + 1) * (l + 1) - 1
            last = m == l * l
            g_codes, g_scales = g_packed_of_row[m]
            for t in range(c0 // P, c1 // P):
                if first:
                    acc_of_tile[(l, t)] = banks.tile([P, C_OUT], F32, name="acc%d" % t, tag="acc")
                columns = slice(t * P - c0, (t + 1) * P - c0)
                nc.tensor.matmul_mx(
                    out=acc_of_tile[(l, t)][:],
                    lhsT=x_codes[:, columns].bitcast(E4M3_X4),
                    lhsT_scale=x_scales[:, columns],
                    rhs=g_codes[:].bitcast(E5M2_X4),
                    rhs_scale=g_scales[:],
                    start=first,
                    stop=last,
                )

        def drain(l, t0):
            n = STORE_TILES[l]
            staged = staging.tile([P, n, C_OUT], F32, tag="staged%d" % n, bufs=STAGED_BUFS[n])
            for t in range(n):
                acc = acc_of_tile[(l, t0 + t)]
                if t0 + t in VECTOR_TILES[l]:
                    nc.vector.tensor_scalar_mul(out=staged[:, t, :], in0=acc[:], scalar1=pw[:, l : l + 1])
                else:
                    nc.scalar.activation(out=staged[:, t, :], in_=acc[:], func=COPY, scale=pw[:, l : l + 1])
            nc.sync.dma_start(out=out[l].rearrange("(q p t) j -> p q t j", p=P, t=n)[:, t0 // n], in_=staged[:])

        ctx.enter_context(tc.manual_schedule())

        scalar_done = 0
        vector_done = 0
        finished = []

        load_up_to(2)
        nc.sync.dma_start(out=pw_bf16[:], in_=path_weights.partition_broadcast(P))
        load_up_to(4)
        for i, (m, c0, c1) in enumerate(steps):
            load_up_to(i + 1 + LOAD_LEAD)
            while scalar_done < min(i + 1 + SCALAR_LEAD, len(steps)):
                regroup_x_scalar(scalar_done)
                if scalar_done < len(order):
                    regroup_g(order[scalar_done])
                scalar_done += 1

            if i == 0:
                nc.scalar.copy(out=pw[:], in_=pw_bf16[:])
            if i == 0:
                regroup_x_vector(0)
                x_packed = quantise_x(0)
            if i + 1 < len(steps):
                regroup_x_vector(i + 1)
            if i > 0:
                x_packed = quantise_x(i)
            if i < len(order):
                quantise_g(order[i])
            multiply(i, *x_packed)
            for pair in finished:
                drain(*pair)
            finished = []
            if m == degree_of_row[m] ** 2:
                finished += [(degree_of_row[m], t) for t in range(c0 // P, c1 // P, STORE_TILES[degree_of_row[m]])]

        for pair in finished:
            drain(*pair)
